import numpy as np
import ml_dtypes


def mxq(x, axis, fmt="e4m3"):
    dtype, down = {"e4m3": (ml_dtypes.float8_e4m3fn, 7), "e5m2": (ml_dtypes.float8_e5m2, 14)}[fmt]
    v = np.moveaxis(np.asarray(x, np.float32).astype(ml_dtypes.bfloat16).astype(np.float64), axis, -1)
    blocks = v.reshape(v.shape[:-1] + (-1, 32))
    amax = np.abs(blocks).max(-1, keepdims=True)
    byte = np.maximum(np.where(amax > 0, np.frexp(amax)[1] - 1 + 127, 0) - down, 1)
    scale = np.exp2(byte - 127.0)
    codes = (blocks / scale).astype(np.float32).astype(dtype).astype(np.float64)
    return np.moveaxis((codes * scale).reshape(v.shape), -1, axis)


WIDE = False


def mx_kscale(k):
    if not WIDE:
        return np.ones(k)
    levels = np.array([10, -10, 5, -5, 0])
    a = np.random.permutation(np.resize(levels, k // 512 * 4)).reshape(k // 512, 4)
    idx = np.arange(k)
    return np.exp2(a[idx // 512, idx % 128 // 32])


BF16 = ml_dtypes.bfloat16


def bf(x):
    return np.asarray(x, np.float32).astype(BF16)


def f64(x):
    return np.asarray(x).astype(np.float64)


E2M1 = np.array([0.0, 0.5, 1.0, 1.5, 2.0, 3.0, 4.0, 6.0, -0.0, -0.5, -1.0, -1.5, -2.0, -3.0, -4.0, -6.0])


def pack_weight(w, fmt):
    k, n = w.shape
    w = f64(bf(w)).reshape(k // 32, 32, n)
    amax = np.abs(w).max(1)
    if fmt == "e4m3":
        byte = np.frexp(amax)[1] - 1 + 127 - 7
    else:
        mant, ex = np.frexp(amax / 6.0)
        byte = np.where(mant > 0.5, ex, ex - 1) + 127
    byte = np.clip(np.where(amax > 0, byte, 1), 1, 254)
    scaled = (w * np.exp2(127.0 - byte)[:, None, :]).reshape(k, n).astype(np.float32)
    by_word = np.ascontiguousarray(scaled.reshape(k // 512, 128, 4, n).transpose(0, 1, 3, 2))
    if fmt == "e4m3":
        words = by_word.astype(ml_dtypes.float8_e4m3fn).view(np.uint8)
    else:
        c = by_word.astype(ml_dtypes.float4_e2m1fn).view(np.uint8) & 0xF
        words = c[..., 0::2] | (c[..., 1::2] << 4)
    return np.ascontiguousarray(words), np.ascontiguousarray(byte.astype(np.uint8).reshape(k // 512, 16, n))


def unpack_weight(words, scales, fmt):
    g, p, n, _ = words.shape
    if fmt == "e4m3":
        vals = np.ascontiguousarray(words).view(ml_dtypes.float8_e4m3fn).astype(np.float64)
    else:
        nib = np.empty((g, p, n, 4), np.uint8)
        nib[..., 0::2] = words & 0xF
        nib[..., 1::2] = words >> 4
        vals = E2M1[nib]
    vals = vals * np.repeat(np.exp2(scales.astype(np.float64) - 127.0), 8, axis=1)[..., None]
    return vals.transpose(0, 1, 3, 2).reshape(g * 512, n)


B, IMG, P0, P1, C, F = 8, 128, 16, 32, 4, 4096
E0, E1 = IMG // P0, IMG // P1
N0, N1 = E0 * E0, E1 * E1
D0, D1 = P0 * P0 * C, P1 * P1 * C


def setup_inputs():
    s = mx_kscale(D1)
    flat = np.random.standard_normal((B, N1, D1)) * s
    img = flat.reshape(B, E1, E1, P1, P1, C).transpose(0, 1, 3, 2, 4, 5).reshape(B, IMG, IMG, C)
    encoded = img.reshape(B, E0, P0, E0, P0, C).transpose(0, 1, 3, 2, 4, 5).reshape(B, N0, D0)
    words, scales = pack_weight(np.random.standard_normal((D1, F)) / np.sqrt(D1) / s[:, None], "e4m3")
    return {"encoded": bf(encoded),
            "W_words": words,
            "W_scales": scales,
            "b": bf(np.random.standard_normal(F) * 0.3),
            "pos_emb": bf(np.random.standard_normal((N1, F)) * 0.5)}


def reference(encoded, W_words, W_scales, b, pos_emb):
    x = f64(encoded).reshape(-1, E0, E0, P0, P0, C)
    img = x.transpose(0, 1, 3, 2, 4, 5).reshape(-1, IMG, IMG, C)
    new_patches = img.reshape(-1, E1, P1, E1, P1, C).transpose(0, 1, 3, 2, 4, 5)
    flat = new_patches.reshape(-1, N1, D1)
    return (mxq(flat, 2, "e4m3") @ unpack_weight(W_words, W_scales, "e4m3")) + f64(b) + f64(pos_emb)

@@ -1,0 +1,146 @@
+from contextlib import ExitStack
+
+import concourse.mybir as mybir
+from concourse.masks import make_identity
+
+F32 = mybir.dt.float32
+BF16 = mybir.dt.bfloat16
+I32 = mybir.dt.int32
+U32 = mybir.dt.uint32
+U8 = mybir.dt.uint8
+FP8X4 = mybir.dt.float8_e4m3fn_x4
+ADD = mybir.AluOpType.add
+
+P = 128
+K = 4096
+F = 4096
+G = 8
+NB = 512
+FLOPS = 2 * P * K * F
+
+LAST_PIECES = [(0, 1024), (1024, 2048), (2048, 3072), (3072, 3584), (3584, 4096)]
+
+
+def tile_resampling_w_kernel(tc, encoded, W_words, W_scales, b, pos_emb, out):
+    nc = tc.nc
+    with ExitStack() as ctx:
+        ctx.enter_context(tc.manual_schedule())
+        keep = ctx.enter_context(tc.tile_pool(name="keep", bufs=1))
+        psum = ctx.enter_context(tc.psum_pool(name="psum", bufs=1))
+
+        x_sb = keep.tile([P, 2, 2048], BF16, name="x_sb")
+        x_sorted = keep.tile([P, 2, 2, 512], F32, name="x_sorted")
+        grouped = keep.tile([P, G, P, 4], BF16, name="grouped", align_bytes=64)
+        x_codes = keep.tile([P, G * P], U32, name="x_codes", align_bytes=64)
+        x_scl = keep.tile([P, G * P], U8, name="x_scl", align_bytes=64)
+        planes = keep.tile([P, 2, F], U8, name="planes", align_bytes=64)
+        w_sb = [keep.tile([P, F], U32, name="w%d" % g, align_bytes=64) for g in range(G)]
+        ident_f = keep.tile([P, P], F32, name="ident_f")
+        ident_b = keep.tile([P, P], BF16, name="ident_b")
+        spread = keep.tile([P, 8, 8, 16], BF16, name="spread")
+        pos_sb = keep.tile([P, NB], BF16, name="pos_sb")
+        b_sb = keep.tile([P, NB], BF16, name="b_sb")
+        res = keep.tile([P, F], F32, name="res")
+
+        x_src = encoded.rearrange("i (Y yh X xh) d -> yh (i Y) X (xh d)", Y=4, yh=2, X=4, xh=2)
+        for yh in range(2):
+            nc.sync.dma_start(out=x_sb[:, yh, :], in_=x_src[yh])
+        nc.scalar.dma_start(out=pos_sb[:], in_=pos_emb.rearrange("a (c n) -> (a c) n", c=8))
+        nc.vector.memset(planes[:].rearrange("p h n -> p (h n)").bitcast(I32), 0)
+        nc.vector.memset(b_sb[:], 0.0)
+        nc.scalar.dma_start(out=b_sb[0:8, :], in_=b.rearrange("(c n) -> c n", c=8))
+        for h in range(2):
+            for q in range(4):
+                nc.sync.dma_start(
+                    out=planes[32 * q : 32 * q + 16, h, :].bitcast(I32),
+                    in_=W_scales[4 * h : 4 * h + 4, 4 * q : 4 * q + 4, :].bitcast(I32),
+                )
+        for g in range(G - 1):
+            nc.sync.dma_start(
+                out=w_sb[g][:].bitcast(I32),
+                in_=W_words[g].rearrange("p n t -> p (n t)").bitcast(I32),
+            )
+        w_last = W_words[G - 1].rearrange("p n t -> p (n t)")
+        for c0, c1 in LAST_PIECES:
+            nc.sync.dma_start(
+                out=w_sb[G - 1][:, c0:c1].bitcast(I32),
+                in_=w_last[:, 4 * c0 : 4 * c1].bitcast(I32),
+            )
+
+        make_identity(nc, ident_f[:])
+        make_identity(nc, ident_b[:])
+        nc.vector.tensor_copy(
+            out=spread[:],
+            in_=ident_b[:].rearrange("k (a c) -> k c a", c=8).unsqueeze(2).to_broadcast([P, 8, 8, 16]),
+        )
+
+        x_words = x_sb[:].bitcast(F32).rearrange(
+            "m yh (xh y x u) -> m yh u y xh x", xh=2, y=16, x=16, u=2
+        )
+        for yh in range(2):
+            for u in range(2):
+                dst = x_sorted[:, u, yh, :].rearrange("m (y xh x) -> m y xh x", y=16, xh=2, x=16)
+                if u == 0:
+                    nc.vector.tensor_copy(out=dst, in_=x_words[:, yh, u])
+                else:
+                    nc.scalar.copy(out=dst, in_=x_words[:, yh, u])
+        grouped_w = (
+            grouped[:].rearrange("p g m t -> p (g m t)").bitcast(F32).rearrange("p (g m u) -> p g m u", g=G, m=P, u=2)
+        )
+        xts = []
+        for j in range(4):
+            xt = psum.tile([P, 2, 2, P], F32, name="xt%d" % j, tag="bank%d" % j)
+            xts.append(xt)
+            for gl in range(2):
+                g = 2 * j + gl
+                for u in range(2):
+                    nc.tensor.transpose(
+                        xt[:, gl, u, :],
+                        x_sorted[:, u, g // 4, (g % 4) * P : (g % 4 + 1) * P],
+                        ident_f[:],
+                    )
+        for j in range(4):
+            src = xts[j][:].rearrange("p g u m -> p g m u")
+            if j % 2 == 0:
+                nc.vector.tensor_copy(out=grouped_w[:, 2 * j : 2 * j + 2], in_=src)
+            else:
+                nc.scalar.copy(out=grouped_w[:, 2 * j : 2 * j + 2], in_=src)
+        grouped_flat = grouped[:].rearrange("p g m t -> p (g m t)")
+        for h in range(2):
+            nc.vector.quantize_mx(
+                out=x_codes[:, 512 * h : 512 * (h + 1)].bitcast(FP8X4),
+                scales=x_scl[:, 512 * h : 512 * (h + 1)],
+                in_=grouped_flat[:, 2048 * h : 2048 * (h + 1)],
+            )
+
+        for c in range(8):
+            bb = psum.tile([P, NB], F32, name="bb%d" % c, tag="bank%d" % ((c + 4) % 8))
+            nc.tensor.matmul(
+                bb[:], lhsT=spread[:, c].rearrange("k i a -> k (i a)"), rhs=pos_sb[:], start=True, stop=False
+            )
+            nc.tensor.matmul(
+                bb[:], lhsT=ident_b[:, c : c + 1].to_broadcast([P, P]), rhs=b_sb[:], start=False, stop=True
+            )
+            nc.scalar.copy(out=res[:, c * NB : (c + 1) * NB], in_=bb[:])
+
+        acc = [psum.tile([P, NB], F32, name="acc%d" % j, tag="bank%d" % ((j + 4) % 8)) for j in range(8)]
+        for g in range(G):
+            k = 4 * (g % 4)
+            for j in range(8):
+                cols = slice(j * NB, (j + 1) * NB)
+                nc.tensor.matmul_mx(
+                    out=acc[j][:],
+                    lhsT=x_codes[:, g * P : (g + 1) * P].bitcast(FP8X4),
+                    lhsT_scale=x_scl[:, g * P : (g + 1) * P],
+                    rhs=w_sb[g][:, cols].bitcast(FP8X4),
+                    rhs_scale=planes[k:P, g // 4, cols],
+                    start=(g == 0),
+                    stop=(g == G - 1),
+                )
+
+        out_flat = out.rearrange("i a n -> (i a) n")
+        for c0, c1 in LAST_PIECES:
+            for j in range(c0 // NB, c1 // NB):
+                cols = slice(j * NB, (j + 1) * NB)
+                nc.vector.tensor_tensor(out=res[:, cols], in0=acc[j][:], in1=res[:, cols], op=ADD)
+            nc.sync.dma_start(out=out_flat[:, c0:c1], in_=res[:, c0:c1])

@@ -49,12 +49,6 @@ def tile_resampling_w_kernel(tc, encoded, W_words, W_scales, b, pos_emb, out):
         nc.vector.memset(planes[:].rearrange("p h n -> p (h n)").bitcast(I32), 0)
         nc.vector.memset(b_sb[:], 0.0)
         nc.scalar.dma_start(out=b_sb[0:8, :], in_=b.rearrange("(c n) -> c n", c=8))
-        for h in range(2):
-            for q in range(4):
-                nc.sync.dma_start(
-                    out=planes[32 * q : 32 * q + 16, h, :].bitcast(I32),
-                    in_=W_scales[4 * h : 4 * h + 4, 4 * q : 4 * q + 4, :].bitcast(I32),
-                )
         for g in range(G - 1):
             nc.sync.dma_start(
                 out=w_sb[g][:].bitcast(I32),
@@ -69,6 +63,12 @@ def tile_resampling_w_kernel(tc, encoded, W_words, W_scales, b, pos_emb, out):
 
         make_identity(nc, ident_f[:])
         make_identity(nc, ident_b[:])
+        for h in range(2):
+            for q in (0, 2, 1, 3):
+                nc.gpsimd.dma_start(
+                    out=planes[32 * q : 32 * q + 16, h, :].bitcast(F32),
+                    in_=W_scales[4 * h : 4 * h + 4, 4 * q : 4 * q + 4, :].bitcast(F32),
+                )
         nc.vector.tensor_copy(
             out=spread[:],
             in_=ident_b[:].rearrange("k (a c) -> k c a", c=8).unsqueeze(2).to_broadcast([P, 8, 8, 16]),

@@ -18,6 +18,8 @@ G = 8
 NB = 512
 FLOPS = 2 * P * K * F
 
+WHOLE = 5
+HALVES = [(0, 2048), (2048, 4096)]
 LAST_PIECES = [(0, 1024), (1024, 2048), (2048, 3072), (3072, 3584), (3584, 4096)]
 
 
@@ -49,26 +51,24 @@ def tile_resampling_w_kernel(tc, encoded, W_words, W_scales, b, pos_emb, out):
         nc.vector.memset(planes[:].rearrange("p h n -> p (h n)").bitcast(I32), 0)
         nc.vector.memset(b_sb[:], 0.0)
         nc.scalar.dma_start(out=b_sb[0:8, :], in_=b.rearrange("(c n) -> c n", c=8))
-        for g in range(G - 1):
-            nc.sync.dma_start(
-                out=w_sb[g][:].bitcast(I32),
-                in_=W_words[g].rearrange("p n t -> p (n t)").bitcast(I32),
-            )
-        w_last = W_words[G - 1].rearrange("p n t -> p (n t)")
+        for h in range(2):
+            for q in range(4):
+                nc.sync.dma_start(
+                    out=planes[32 * q : 32 * q + 16, h, :].bitcast(I32),
+                    in_=W_scales[4 * h : 4 * h + 4, 4 * q : 4 * q + 4, :].bitcast(I32),
+                )
+        cells = [(g, 0, F) for g in range(WHOLE)]
+        cells += [(WHOLE, c0, c1) for c0, c1 in HALVES]
         for c0, c1 in LAST_PIECES:
+            cells += [(g, c0, c1) for g in range(WHOLE + 1, G)]
+        for g, c0, c1 in cells:
             nc.sync.dma_start(
-                out=w_sb[G - 1][:, c0:c1].bitcast(I32),
-                in_=w_last[:, 4 * c0 : 4 * c1].bitcast(I32),
+                out=w_sb[g][:, c0:c1].bitcast(I32),
+                in_=W_words[g].rearrange("p n t -> p (n t)")[:, 4 * c0 : 4 * c1].bitcast(I32),
             )
 
         make_identity(nc, ident_f[:])
         make_identity(nc, ident_b[:])
-        for h in range(2):
-            for q in (0, 2, 1, 3):
-                nc.gpsimd.dma_start(
-                    out=planes[32 * q : 32 * q + 16, h, :].bitcast(F32),
-                    in_=W_scales[4 * h : 4 * h + 4, 4 * q : 4 * q + 4, :].bitcast(F32),
-                )
         nc.vector.tensor_copy(
             out=spread[:],
             in_=ident_b[:].rearrange("k (a c) -> k c a", c=8).unsqueeze(2).to_broadcast([P, 8, 8, 16]),
@@ -124,9 +124,9 @@ def tile_resampling_w_kernel(tc, encoded, W_words, W_scales, b, pos_emb, out):
             nc.scalar.copy(out=res[:, c * NB : (c + 1) * NB], in_=bb[:])
 
         acc = [psum.tile([P, NB], F32, name="acc%d" % j, tag="bank%d" % ((j + 4) % 8)) for j in range(8)]
-        for g in range(G):
+        for g, c0, c1 in cells:
             k = 4 * (g % 4)
-            for j in range(8):
+            for j in range(c0 // NB, c1 // NB):
                 cols = slice(j * NB, (j + 1) * NB)
                 nc.tensor.matmul_mx(
                     out=acc[j][:],

@@ -18,8 +18,8 @@ G = 8
 NB = 512
 FLOPS = 2 * P * K * F
 
-WHOLE = 5
-HALVES = [(0, 2048), (2048, 4096)]
+WHOLE = 6
+STORES = [(0, 2048), (2048, 3072), (3072, 3584), (3584, 4096)]
 LAST_PIECES = [(0, 1024), (1024, 2048), (2048, 3072), (3072, 3584), (3584, 4096)]
 
 
@@ -36,7 +36,7 @@ def tile_resampling_w_kernel(tc, encoded, W_words, W_scales, b, pos_emb, out):
         x_codes = keep.tile([P, G * P], U32, name="x_codes", align_bytes=64)
         x_scl = keep.tile([P, G * P], U8, name="x_scl", align_bytes=64)
         planes = keep.tile([P, 2, F], U8, name="planes", align_bytes=64)
-        w_sb = [keep.tile([P, F], U32, name="w%d" % g, align_bytes=64) for g in range(G)]
+        w_all = keep.tile([P, G, F], U32, name="w_all", align_bytes=64)
         ident_f = keep.tile([P, P], F32, name="ident_f")
         ident_b = keep.tile([P, P], BF16, name="ident_b")
         spread = keep.tile([P, 8, 8, 16], BF16, name="spread")
@@ -47,23 +47,27 @@ def tile_resampling_w_kernel(tc, encoded, W_words, W_scales, b, pos_emb, out):
         x_src = encoded.rearrange("i (Y yh X xh) d -> yh (i Y) X (xh d)", Y=4, yh=2, X=4, xh=2)
         for yh in range(2):
             nc.sync.dma_start(out=x_sb[:, yh, :], in_=x_src[yh])
-        nc.scalar.dma_start(out=pos_sb[:], in_=pos_emb.rearrange("a (c n) -> (a c) n", c=8))
-        nc.vector.memset(planes[:].rearrange("p h n -> p (h n)").bitcast(I32), 0)
+        nc.sync.dma_start(out=pos_sb[:], in_=pos_emb.rearrange("a (c n) -> (a c) n", c=8))
         nc.vector.memset(b_sb[:], 0.0)
-        nc.scalar.dma_start(out=b_sb[0:8, :], in_=b.rearrange("(c n) -> c n", c=8))
+        nc.vector.memset(planes[:].rearrange("p h n -> p (h n)").bitcast(I32), 0)
+        nc.sync.dma_start(out=b_sb[0:8, :], in_=b.rearrange("(c n) -> c n", c=8))
         for h in range(2):
             for q in range(4):
                 nc.sync.dma_start(
                     out=planes[32 * q : 32 * q + 16, h, :].bitcast(I32),
                     in_=W_scales[4 * h : 4 * h + 4, 4 * q : 4 * q + 4, :].bitcast(I32),
                 )
-        cells = [(g, 0, F) for g in range(WHOLE)]
-        cells += [(WHOLE, c0, c1) for c0, c1 in HALVES]
-        for c0, c1 in LAST_PIECES:
-            cells += [(g, c0, c1) for g in range(WHOLE + 1, G)]
-        for g, c0, c1 in cells:
+        for g in (0, 2):
             nc.sync.dma_start(
-                out=w_sb[g][:, c0:c1].bitcast(I32),
+                out=w_all[:, g : g + 2, :].bitcast(I32),
+                in_=W_words[g : g + 2].rearrange("g p n t -> p g (n t)").bitcast(I32),
+            )
+        cells = [(g, 0, F) for g in range(WHOLE)]
+        for c0, c1 in LAST_PIECES:
+            cells += [(g, c0, c1) for g in range(WHOLE, G)]
+        for g, c0, c1 in cells[4:]:
+            nc.sync.dma_start(
+                out=w_all[:, g, c0:c1].bitcast(I32),
                 in_=W_words[g].rearrange("p n t -> p (n t)")[:, 4 * c0 : 4 * c1].bitcast(I32),
             )
 
@@ -132,14 +136,14 @@ def tile_resampling_w_kernel(tc, encoded, W_words, W_scales, b, pos_emb, out):
                     out=acc[j][:],
                     lhsT=x_codes[:, g * P : (g + 1) * P].bitcast(FP8X4),
                     lhsT_scale=x_scl[:, g * P : (g + 1) * P],
-                    rhs=w_sb[g][:, cols].bitcast(FP8X4),
+                    rhs=w_all[:, g, cols].bitcast(FP8X4),
                     rhs_scale=planes[k:P, g // 4, cols],
                     start=(g == 0),
                     stop=(g == G - 1),
                 )
 
         out_flat = out.rearrange("i a n -> (i a) n")
-        for c0, c1 in LAST_PIECES:
+        for c0, c1 in STORES:
             for j in range(c0 // NB, c1 // NB):
                 cols = slice(j * NB, (j + 1) * NB)
                 nc.vector.tensor_tensor(out=res[:, cols], in0=acc[j][:], in1=res[:, cols], op=ADD)

@@ -21,6 +21,7 @@ FLOPS = 2 * P * K * F
 WHOLE = 6
 STORES = [(0, 2048), (2048, 3072), (3072, 3584), (3584, 4096)]
 LAST_PIECES = [(0, 1024), (1024, 2048), (2048, 3072), (3072, 3584), (3584, 4096)]
+EARLY_LOADS = [(0, 3), (3, 5), (5, 6)]
 
 
 def tile_resampling_w_kernel(tc, encoded, W_words, W_scales, b, pos_emb, out):
@@ -30,7 +31,7 @@ def tile_resampling_w_kernel(tc, encoded, W_words, W_scales, b, pos_emb, out):
         keep = ctx.enter_context(tc.tile_pool(name="keep", bufs=1))
         psum = ctx.enter_context(tc.psum_pool(name="psum", bufs=1))
 
-        x_sb = keep.tile([P, 2, 2048], BF16, name="x_sb")
+        x_sb = keep.tile([P, K], BF16, name="x_sb")
         x_sorted = keep.tile([P, 2, 2, 512], F32, name="x_sorted")
         grouped = keep.tile([P, G, P, 4], BF16, name="grouped", align_bytes=64)
         x_codes = keep.tile([P, G * P], U32, name="x_codes", align_bytes=64)
@@ -44,31 +45,22 @@ def tile_resampling_w_kernel(tc, encoded, W_words, W_scales, b, pos_emb, out):
         b_sb = keep.tile([P, NB], BF16, name="b_sb")
         res = keep.tile([P, F], F32, name="res")
 
-        x_src = encoded.rearrange("i (Y yh X xh) d -> yh (i Y) X (xh d)", Y=4, yh=2, X=4, xh=2)
-        for yh in range(2):
-            nc.sync.dma_start(out=x_sb[:, yh, :], in_=x_src[yh])
+        nc.sync.dma_start(out=x_sb[:], in_=encoded.rearrange("i (a t) d -> (i a) (t d)", t=4))
         nc.sync.dma_start(out=pos_sb[:], in_=pos_emb.rearrange("a (c n) -> (a c) n", c=8))
         nc.vector.memset(b_sb[:], 0.0)
         nc.vector.memset(planes[:].rearrange("p h n -> p (h n)").bitcast(I32), 0)
         nc.sync.dma_start(out=b_sb[0:8, :], in_=b.rearrange("(c n) -> c n", c=8))
         for h in range(2):
-            for q in range(4):
+            for q in (0, 2, 1, 3):
                 nc.sync.dma_start(
                     out=planes[32 * q : 32 * q + 16, h, :].bitcast(I32),
                     in_=W_scales[4 * h : 4 * h + 4, 4 * q : 4 * q + 4, :].bitcast(I32),
                 )
-        for g in (0, 2):
+        loads = [(g0, g1, 0, F) for g0, g1 in EARLY_LOADS] + [(WHOLE, G, c0, c1) for c0, c1 in LAST_PIECES]
+        for g0, g1, c0, c1 in loads:
             nc.sync.dma_start(
-                out=w_all[:, g : g + 2, :].bitcast(I32),
-                in_=W_words[g : g + 2].rearrange("g p n t -> p g (n t)").bitcast(I32),
-            )
-        cells = [(g, 0, F) for g in range(WHOLE)]
-        for c0, c1 in LAST_PIECES:
-            cells += [(g, c0, c1) for g in range(WHOLE, G)]
-        for g, c0, c1 in cells[4:]:
-            nc.sync.dma_start(
-                out=w_all[:, g, c0:c1].bitcast(I32),
-                in_=W_words[g].rearrange("p n t -> p (n t)")[:, 4 * c0 : 4 * c1].bitcast(I32),
+                out=w_all[:, g0:g1, c0:c1].bitcast(I32),
+                in_=W_words[g0:g1].rearrange("g p n t -> p g (n t)")[:, :, 4 * c0 : 4 * c1].bitcast(I32),
             )
 
         make_identity(nc, ident_f[:])
@@ -79,36 +71,39 @@ def tile_resampling_w_kernel(tc, encoded, W_words, W_scales, b, pos_emb, out):
         )
 
         x_words = x_sb[:].bitcast(F32).rearrange(
-            "m yh (xh y x u) -> m yh u y xh x", xh=2, y=16, x=16, u=2
+            "m (xl xh y x u) -> m xl u y xh x", xl=2, xh=2, y=16, x=16, u=2
         )
-        for yh in range(2):
+        for xl in range(2):
             for u in range(2):
-                dst = x_sorted[:, u, yh, :].rearrange("m (y xh x) -> m y xh x", y=16, xh=2, x=16)
+                dst = x_sorted[:, u, xl, :].rearrange("m (y xh x) -> m y xh x", y=16, xh=2, x=16)
                 if u == 0:
-                    nc.vector.tensor_copy(out=dst, in_=x_words[:, yh, u])
+                    nc.vector.tensor_copy(out=dst, in_=x_words[:, xl, u])
                 else:
-                    nc.scalar.copy(out=dst, in_=x_words[:, yh, u])
+                    nc.scalar.copy(out=dst, in_=x_words[:, xl, u])
         grouped_w = (
-            grouped[:].rearrange("p g m t -> p (g m t)").bitcast(F32).rearrange("p (g m u) -> p g m u", g=G, m=P, u=2)
+            grouped[:]
+            .rearrange("p g m t -> p (g m t)")
+            .bitcast(F32)
+            .rearrange("p (g iy xhi c) -> p g iy xhi c", g=G, iy=32, xhi=2, c=4)
         )
         xts = []
-        for j in range(4):
-            xt = psum.tile([P, 2, 2, P], F32, name="xt%d" % j, tag="bank%d" % j)
+        for g4 in range(4):
+            xt = psum.tile([P, 4, P], F32, name="xt%d" % g4, tag="bank%d" % g4)
             xts.append(xt)
-            for gl in range(2):
-                g = 2 * j + gl
+            for xl in range(2):
                 for u in range(2):
                     nc.tensor.transpose(
-                        xt[:, gl, u, :],
-                        x_sorted[:, u, g // 4, (g % 4) * P : (g % 4 + 1) * P],
+                        xt[:, 2 * xl + u, :],
+                        x_sorted[:, u, xl, g4 * P : (g4 + 1) * P],
                         ident_f[:],
                     )
-        for j in range(4):
-            src = xts[j][:].rearrange("p g u m -> p g m u")
-            if j % 2 == 0:
-                nc.vector.tensor_copy(out=grouped_w[:, 2 * j : 2 * j + 2], in_=src)
-            else:
-                nc.scalar.copy(out=grouped_w[:, 2 * j : 2 * j + 2], in_=src)
+        for yh in range(2):
+            for g4 in range(4):
+                src = xts[g4][:].rearrange("p c (iy yh xhi) -> p yh iy xhi c", iy=32, yh=2, xhi=2)[:, yh]
+                if g4 % 2 == 0:
+                    nc.vector.tensor_copy(out=grouped_w[:, 4 * yh + g4], in_=src)
+                else:
+                    nc.scalar.copy(out=grouped_w[:, 4 * yh + g4], in_=src)
         grouped_flat = grouped[:].rearrange("p g m t -> p (g m t)")
         for h in range(2):
             nc.vector.quantize_mx(
@@ -128,6 +123,9 @@ def tile_resampling_w_kernel(tc, encoded, W_words, W_scales, b, pos_emb, out):
             nc.scalar.copy(out=res[:, c * NB : (c + 1) * NB], in_=bb[:])
 
         acc = [psum.tile([P, NB], F32, name="acc%d" % j, tag="bank%d" % ((j + 4) % 8)) for j in range(8)]
+        cells = [(g, 0, F) for g in range(WHOLE)]
+        for c0, c1 in LAST_PIECES:
+            cells += [(g, c0, c1) for g in range(WHOLE, G)]
         for g, c0, c1 in cells:
             k = 4 * (g % 4)
             for j in range(c0 // NB, c1 // NB):

@@ -46,10 +46,10 @@ def tile_resampling_w_kernel(tc, encoded, W_words, W_scales, b, pos_emb, out):
         res = keep.tile([P, F], F32, name="res")
 
         nc.sync.dma_start(out=x_sb[:], in_=encoded.rearrange("i (a t) d -> (i a) (t d)", t=4))
-        nc.sync.dma_start(out=pos_sb[:], in_=pos_emb.rearrange("a (c n) -> (a c) n", c=8))
+        nc.scalar.dma_start(out=pos_sb[:], in_=pos_emb.rearrange("a (c n) -> (a c) n", c=8))
         nc.vector.memset(b_sb[:], 0.0)
         nc.vector.memset(planes[:].rearrange("p h n -> p (h n)").bitcast(I32), 0)
-        nc.sync.dma_start(out=b_sb[0:8, :], in_=b.rearrange("(c n) -> c n", c=8))
+        nc.scalar.dma_start(out=b_sb[0:8, :], in_=b.rearrange("(c n) -> c n", c=8))
         for h in range(2):
             for q in (0, 2, 1, 3):
                 nc.sync.dma_start(

@@ -50,8 +50,8 @@ def tile_resampling_w_kernel(tc, encoded, W_words, W_scales, b, pos_emb, out):
         nc.vector.memset(b_sb[:], 0.0)
         nc.vector.memset(planes[:].rearrange("p h n -> p (h n)").bitcast(I32), 0)
         nc.scalar.dma_start(out=b_sb[0:8, :], in_=b.rearrange("(c n) -> c n", c=8))
-        for h in range(2):
-            for q in (0, 2, 1, 3):
+        for h, q in [(0, 2), (0, 3), (1, 2), (1, 3), (0, 0), (0, 1), (1, 0), (1, 1)]:
+            if True:
                 nc.sync.dma_start(
                     out=planes[32 * q : 32 * q + 16, h, :].bitcast(I32),
                     in_=W_scales[4 * h : 4 * h + 4, 4 * q : 4 * q + 4, :].bitcast(I32),

@@ -19,9 +19,16 @@ NB = 512
 FLOPS = 2 * P * K * F
 
 WHOLE = 6
-STORES = [(0, 2048), (2048, 3072), (3072, 3584), (3584, 4096)]
-LAST_PIECES = [(0, 1024), (1024, 2048), (2048, 3072), (3072, 3584), (3584, 4096)]
-EARLY_LOADS = [(0, 3), (3, 5), (5, 6)]
+STORES = [(0, 1024), (1024, 2048), (2048, 3072), (3072, 3584), (3584, 4096)]
+LOADS = [
+    (0, 3, 0, 4096),
+    (3, 5, 0, 4096),
+    (5, 6, 0, 4096),
+    (6, 8, 0, 2048),
+    (6, 8, 2048, 3072),
+    (6, 7, 3072, 4096),
+    (7, 8, 3072, 4096),
+]
 
 
 def tile_resampling_w_kernel(tc, encoded, W_words, W_scales, b, pos_emb, out):
@@ -56,8 +63,7 @@ def tile_resampling_w_kernel(tc, encoded, W_words, W_scales, b, pos_emb, out):
                     out=planes[32 * q : 32 * q + 16, h, :].bitcast(I32),
                     in_=W_scales[4 * h : 4 * h + 4, 4 * q : 4 * q + 4, :].bitcast(I32),
                 )
-        loads = [(g0, g1, 0, F) for g0, g1 in EARLY_LOADS] + [(WHOLE, G, c0, c1) for c0, c1 in LAST_PIECES]
-        for g0, g1, c0, c1 in loads:
+        for g0, g1, c0, c1 in LOADS:
             nc.sync.dma_start(
                 out=w_all[:, g0:g1, c0:c1].bitcast(I32),
                 in_=W_words[g0:g1].rearrange("g p n t -> p g (n t)")[:, :, 4 * c0 : 4 * c1].bitcast(I32),
@@ -123,12 +129,15 @@ def tile_resampling_w_kernel(tc, encoded, W_words, W_scales, b, pos_emb, out):
             nc.scalar.copy(out=res[:, c * NB : (c + 1) * NB], in_=bb[:])
 
         acc = [psum.tile([P, NB], F32, name="acc%d" % j, tag="bank%d" % ((j + 4) % 8)) for j in range(8)]
-        cells = [(g, 0, F) for g in range(WHOLE)]
-        for c0, c1 in LAST_PIECES:
-            cells += [(g, c0, c1) for g in range(WHOLE, G)]
-        for g, c0, c1 in cells:
+        cells = []
+        for g0, g1, c0, c1 in LOADS:
+            if g0 < WHOLE:
+                cells += [(g, j) for g in range(g0, g1) for j in range(c0 // NB, c1 // NB)]
+            else:
+                cells += [(g, j) for j in range(c0 // NB, c1 // NB) for g in range(g0, g1)]
+        for g, j in cells:
             k = 4 * (g % 4)
-            for j in range(c0 // NB, c1 // NB):
+            if True:
                 cols = slice(j * NB, (j + 1) * NB)
                 nc.tensor.matmul_mx(
                     out=acc[j][:],

@@ -57,17 +57,14 @@ def tile_resampling_w_kernel(tc, encoded, W_words, W_scales, b, pos_emb, out):
         nc.vector.memset(b_sb[:], 0.0)
         nc.vector.memset(planes[:].rearrange("p h n -> p (h n)").bitcast(I32), 0)
         nc.scalar.dma_start(out=b_sb[0:8, :], in_=b.rearrange("(c n) -> c n", c=8))
-        for h, q in [(0, 2), (0, 3), (1, 2), (1, 3), (0, 0), (0, 1), (1, 0), (1, 1)]:
-            if True:
-                nc.sync.dma_start(
-                    out=planes[32 * q : 32 * q + 16, h, :].bitcast(I32),
-                    in_=W_scales[4 * h : 4 * h + 4, 4 * q : 4 * q + 4, :].bitcast(I32),
-                )
-        for g0, g1, c0, c1 in LOADS:
+        def load_scales(h, q):
             nc.sync.dma_start(
-                out=w_all[:, g0:g1, c0:c1].bitcast(I32),
-                in_=W_words[g0:g1].rearrange("g p n t -> p g (n t)")[:, :, 4 * c0 : 4 * c1].bitcast(I32),
+                out=planes[32 * q : 32 * q + 16, h, :].bitcast(I32),
+                in_=W_scales[4 * h : 4 * h + 4, 4 * q : 4 * q + 4, :].bitcast(I32),
             )
+
+        for h, q in [(0, 2), (0, 3), (1, 2), (1, 3), (0, 0), (0, 1)]:
+            load_scales(h, q)
 
         make_identity(nc, ident_f[:])
         make_identity(nc, ident_b[:])
@@ -86,6 +83,16 @@ def tile_resampling_w_kernel(tc, encoded, W_words, W_scales, b, pos_emb, out):
                     nc.vector.tensor_copy(out=dst, in_=x_words[:, xl, u])
                 else:
                     nc.scalar.copy(out=dst, in_=x_words[:, xl, u])
+            if xl == 0:
+                nc.vector.memset(w_all[:, 0, 0:16].bitcast(I32), 0)
+        for g0, g1, c0, c1 in LOADS:
+            nc.sync.dma_start(
+                out=w_all[:, g0:g1, c0:c1].bitcast(I32),
+                in_=W_words[g0:g1].rearrange("g p n t -> p g (n t)")[:, :, 4 * c0 : 4 * c1].bitcast(I32),
+            )
+            if g0 == 0:
+                load_scales(1, 0)
+                load_scales(1, 1)
         grouped_w = (
             grouped[:]
             .rearrange("p g m t -> p (g m t)")

@@ -51,6 +51,7 @@ def tile_resampling_w_kernel(tc, encoded, W_words, W_scales, b, pos_emb, out):
         pos_sb = keep.tile([P, NB], BF16, name="pos_sb")
         b_sb = keep.tile([P, NB], BF16, name="b_sb")
         res = keep.tile([P, F], F32, name="res")
+        scrap = [keep.tile([16, 2, 32], F32, name="scrap%d" % i) for i in range(5)]
 
         nc.sync.dma_start(out=x_sb[:], in_=encoded.rearrange("i (a t) d -> (i a) (t d)", t=4))
         nc.scalar.dma_start(out=pos_sb[:], in_=pos_emb.rearrange("a (c n) -> (a c) n", c=8))
@@ -63,11 +64,21 @@ def tile_resampling_w_kernel(tc, encoded, W_words, W_scales, b, pos_emb, out):
                 in_=W_scales[4 * h : 4 * h + 4, 4 * q : 4 * q + 4, :].bitcast(I32),
             )
 
-        for h, q in [(0, 2), (0, 3), (1, 2), (1, 3), (0, 0), (0, 1)]:
-            load_scales(h, q)
+        for q in range(2):
+            load_scales(0, q)
 
         make_identity(nc, ident_f[:])
         make_identity(nc, ident_b[:])
+        for i, (turn, h, q) in enumerate([(8, 0, 2), (12, 0, 3), (12, 1, 2), (12, 1, 3), (4, None, None)]):
+            nc.gpsimd.dma_start(
+                out=scrap[i][0:turn, :, 0:16],
+                in_=W_scales.bitcast(F32)[0, 0:turn, :].rearrange("q (c n) -> q c n", c=2)[:, :, 0:16],
+            )
+            if h is not None:
+                nc.gpsimd.dma_start(
+                    out=planes[32 * q : 32 * q + 16, h, :].bitcast(F32),
+                    in_=W_scales[4 * h : 4 * h + 4, 4 * q : 4 * q + 4, :].bitcast(F32),
+                )
         nc.vector.tensor_copy(
             out=spread[:],
             in_=ident_b[:].rearrange("k (a c) -> k c a", c=8).unsqueeze(2).to_broadcast([P, 8, 8, 16]),
@@ -83,8 +94,6 @@ def tile_resampling_w_kernel(tc, encoded, W_words, W_scales, b, pos_emb, out):
                     nc.vector.tensor_copy(out=dst, in_=x_words[:, xl, u])
                 else:
                     nc.scalar.copy(out=dst, in_=x_words[:, xl, u])
-            if xl == 0:
-                nc.vector.memset(w_all[:, 0, 0:16].bitcast(I32), 0)
         for g0, g1, c0, c1 in LOADS:
             nc.sync.dma_start(
                 out=w_all[:, g0:g1, c0:c1].bitcast(I32),

from contextlib import ExitStack

import concourse.mybir as mybir
from concourse.masks import make_identity

F32 = mybir.dt.float32
BF16 = mybir.dt.bfloat16
I32 = mybir.dt.int32
U32 = mybir.dt.uint32
U8 = mybir.dt.uint8
FP8X4 = mybir.dt.float8_e4m3fn_x4
ADD = mybir.AluOpType.add

P = 128
K = 4096
F = 4096
G = 8
NB = 512
FLOPS = 2 * P * K * F

WHOLE = 6
STORES = [(0, 1024), (1024, 2048), (2048, 3072), (3072, 3584), (3584, 4096)]
LOADS = [
    (0, 3, 0, 4096),
    (3, 5, 0, 4096),
    (5, 6, 0, 4096),
    (6, 8, 0, 2048),
    (6, 8, 2048, 3072),
    (6, 7, 3072, 4096),
    (7, 8, 3072, 4096),
]


def tile_resampling_w_kernel(tc, encoded, W_words, W_scales, b, pos_emb, out):
    nc = tc.nc
    with ExitStack() as ctx:
        ctx.enter_context(tc.manual_schedule())
        keep = ctx.enter_context(tc.tile_pool(name="keep", bufs=1))
        psum = ctx.enter_context(tc.psum_pool(name="psum", bufs=1))

        x_sb = keep.tile([P, K], BF16, name="x_sb")
        x_sorted = keep.tile([P, 2, 2, 512], F32, name="x_sorted")
        grouped = keep.tile([P, G, P, 4], BF16, name="grouped", align_bytes=64)
        x_codes = keep.tile([P, G * P], U32, name="x_codes", align_bytes=64)
        x_scl = keep.tile([P, G * P], U8, name="x_scl", align_bytes=64)
        planes = keep.tile([P, 2, F], U8, name="planes", align_bytes=64)
        w_all = keep.tile([P, G, F], U32, name="w_all", align_bytes=64)
        ident_f = keep.tile([P, P], F32, name="ident_f")
        ident_b = keep.tile([P, P], BF16, name="ident_b")
        spread = keep.tile([P, 8, 8, 16], BF16, name="spread")
        pos_sb = keep.tile([P, NB], BF16, name="pos_sb")
        b_sb = keep.tile([P, NB], BF16, name="b_sb")
        res = keep.tile([P, F], F32, name="res")
        scrap = [keep.tile([16, 2, 32], F32, name="scrap%d" % i) for i in range(5)]

        nc.sync.dma_start(out=x_sb[:], in_=encoded.rearrange("i (a t) d -> (i a) (t d)", t=4))
        nc.scalar.dma_start(out=pos_sb[:], in_=pos_emb.rearrange("a (c n) -> (a c) n", c=8))
        nc.vector.memset(b_sb[:], 0.0)
        nc.vector.memset(planes[:].rearrange("p h n -> p (h n)").bitcast(I32), 0)
        nc.scalar.dma_start(out=b_sb[0:8, :], in_=b.rearrange("(c n) -> c n", c=8))
        def load_scales(h, q):
            nc.sync.dma_start(
                out=planes[32 * q : 32 * q + 16, h, :].bitcast(I32),
                in_=W_scales[4 * h : 4 * h + 4, 4 * q : 4 * q + 4, :].bitcast(I32),
            )

        for q in range(2):
            load_scales(0, q)

        make_identity(nc, ident_f[:])
        make_identity(nc, ident_b[:])
        for i, (turn, h, q) in enumerate([(8, 0, 2), (12, 0, 3), (12, 1, 2), (12, 1, 3), (4, None, None)]):
            nc.gpsimd.dma_start(
                out=scrap[i][0:turn, :, 0:16],
                in_=W_scales.bitcast(F32)[0, 0:turn, :].rearrange("q (c n) -> q c n", c=2)[:, :, 0:16],
            )
            if h is not None:
                nc.gpsimd.dma_start(
                    out=planes[32 * q : 32 * q + 16, h, :].bitcast(F32),
                    in_=W_scales[4 * h : 4 * h + 4, 4 * q : 4 * q + 4, :].bitcast(F32),
                )
        nc.vector.tensor_copy(
            out=spread[:],
            in_=ident_b[:].rearrange("k (a c) -> k c a", c=8).unsqueeze(2).to_broadcast([P, 8, 8, 16]),
        )

        x_words = x_sb[:].bitcast(F32).rearrange(
            "m (xl xh y x u) -> m xl u y xh x", xl=2, xh=2, y=16, x=16, u=2
        )
        for xl in range(2):
            for u in range(2):
                dst = x_sorted[:, u, xl, :].rearrange("m (y xh x) -> m y xh x", y=16, xh=2, x=16)
                if u == 0:
                    nc.vector.tensor_copy(out=dst, in_=x_words[:, xl, u])
                else:
                    nc.scalar.copy(out=dst, in_=x_words[:, xl, u])
        for g0, g1, c0, c1 in LOADS:
            nc.sync.dma_start(
                out=w_all[:, g0:g1, c0:c1].bitcast(I32),
                in_=W_words[g0:g1].rearrange("g p n t -> p g (n t)")[:, :, 4 * c0 : 4 * c1].bitcast(I32),
            )
            if g0 == 0:
                load_scales(1, 0)
                load_scales(1, 1)
        grouped_w = (
            grouped[:]
            .rearrange("p g m t -> p (g m t)")
            .bitcast(F32)
            .rearrange("p (g iy xhi c) -> p g iy xhi c", g=G, iy=32, xhi=2, c=4)
        )
        xts = []
        for g4 in range(4):
            xt = psum.tile([P, 4, P], F32, name="xt%d" % g4, tag="bank%d" % g4)
            xts.append(xt)
            for xl in range(2):
                for u in range(2):
                    nc.tensor.transpose(
                        xt[:, 2 * xl + u, :],
                        x_sorted[:, u, xl, g4 * P : (g4 + 1) * P],
                        ident_f[:],
                    )
        for yh in range(2):
            for g4 in range(4):
                src = xts[g4][:].rearrange("p c (iy yh xhi) -> p yh iy xhi c", iy=32, yh=2, xhi=2)[:, yh]
                if g4 % 2 == 0:
                    nc.vector.tensor_copy(out=grouped_w[:, 4 * yh + g4], in_=src)
                else:
                    nc.scalar.copy(out=grouped_w[:, 4 * yh + g4], in_=src)
        grouped_flat = grouped[:].rearrange("p g m t -> p (g m t)")
        for h in range(2):
            nc.vector.quantize_mx(
                out=x_codes[:, 512 * h : 512 * (h + 1)].bitcast(FP8X4),
                scales=x_scl[:, 512 * h : 512 * (h + 1)],
                in_=grouped_flat[:, 2048 * h : 2048 * (h + 1)],
            )

        for c in range(8):
            bb = psum.tile([P, NB], F32, name="bb%d" % c, tag="bank%d" % ((c + 4) % 8))
            nc.tensor.matmul(
                bb[:], lhsT=spread[:, c].rearrange("k i a -> k (i a)"), rhs=pos_sb[:], start=True, stop=False
            )
            nc.tensor.matmul(
                bb[:], lhsT=ident_b[:, c : c + 1].to_broadcast([P, P]), rhs=b_sb[:], start=False, stop=True
            )
            nc.scalar.copy(out=res[:, c * NB : (c + 1) * NB], in_=bb[:])

        acc = [psum.tile([P, NB], F32, name="acc%d" % j, tag="bank%d" % ((j + 4) % 8)) for j in range(8)]
        cells = []
        for g0, g1, c0, c1 in LOADS:
            if g0 < WHOLE:
                cells += [(g, j) for g in range(g0, g1) for j in range(c0 // NB, c1 // NB)]
            else:
                cells += [(g, j) for j in range(c0 // NB, c1 // NB) for g in range(g0, g1)]
        for g, j in cells:
            k = 4 * (g % 4)
            if True:
                cols = slice(j * NB, (j + 1) * NB)
                nc.tensor.matmul_mx(
                    out=acc[j][:],
                    lhsT=x_codes[:, g * P : (g + 1) * P].bitcast(FP8X4),
                    lhsT_scale=x_scl[:, g * P : (g + 1) * P],
                    rhs=w_all[:, g, cols].bitcast(FP8X4),
                    rhs_scale=planes[k:P, g // 4, cols],
                    start=(g == 0),
                    stop=(g == G - 1),
                )

        out_flat = out.rearrange("i a n -> (i a) n")
        for c0, c1 in STORES:
            for j in range(c0 // NB, c1 // NB):
                cols = slice(j * NB, (j + 1) * NB)
                nc.vector.tensor_tensor(out=res[:, cols], in0=acc[j][:], in1=res[:, cols], op=ADD)
            nc.sync.dma_start(out=out_flat[:, c0:c1], in_=res[:, c0:c1])
